import numpy as np
import ml_dtypes


def mxq(x, axis, fmt="e4m3"):
    dtype, down = {"e4m3": (ml_dtypes.float8_e4m3fn, 7), "e5m2": (ml_dtypes.float8_e5m2, 14)}[fmt]
    v = np.moveaxis(np.asarray(x, np.float32).astype(ml_dtypes.bfloat16).astype(np.float64), axis, -1)
    blocks = v.reshape(v.shape[:-1] + (-1, 32))
    amax = np.abs(blocks).max(-1, keepdims=True)
    byte = np.maximum(np.where(amax > 0, np.frexp(amax)[1] - 1 + 127, 0) - down, 1)
    scale = np.exp2(byte - 127.0)
    codes = (blocks / scale).astype(np.float32).astype(dtype).astype(np.float64)
    return np.moveaxis((codes * scale).reshape(v.shape), -1, axis)


WIDE = False


def mx_kscale(k):
    if not WIDE:
        return np.ones(k)
    levels = np.array([10, -10, 5, -5, 0])
    a = np.random.permutation(np.resize(levels, k // 512 * 4)).reshape(k // 512, 4)
    idx = np.arange(k)
    return np.exp2(a[idx // 512, idx % 128 // 32])


BF16 = ml_dtypes.bfloat16


def bf(x):
    return np.asarray(x, np.float32).astype(BF16)


def f64(x):
    return np.asarray(x).astype(np.float64)


B, P, L, FI, FO = 512, 2, 3, 512, 256
C = (L + 1) * (L + 1)


def setup_inputs():
    s = mx_kscale(FI)
    return {"x": bf(np.random.standard_normal((B, P, C, FI)) * s),
            "W_e": bf(np.random.standard_normal((L + 1, FI, FO)) / np.sqrt(FI) / s[:, None]),
            "W_o": bf(np.random.standard_normal((L + 1, FI, FO)) / np.sqrt(FI) / s[:, None]),
            "b": bf(np.random.standard_normal(FO) * 0.5)}


def reference(x, W_e, W_o, b):
    xq = mxq(f64(x), 3, "e4m3")
    weq = mxq(f64(W_e), 1, "e4m3")
    woq = mxq(f64(W_o), 1, "e4m3")
    outs_e, outs_o = [], []
    for l in range(L + 1):
        seg = xq[:, :, l * l:(l + 1) * (l + 1), :]
        oe = seg[:, 0] @ weq[l]
        if l == 0:
            oe = oe + f64(b)
        oo = seg[:, 1] @ woq[l]
        outs_e.append(oe)
        outs_o.append(oo)
    return np.stack([np.concatenate(outs_e, axis=-2), np.concatenate(outs_o, axis=-2)], axis=-3)

@@ -1,0 +1,194 @@
+from contextlib import ExitStack
+
+import concourse.mybir as mybir
+from concourse.masks import make_identity
+
+F32 = mybir.dt.float32
+BF16 = mybir.dt.bfloat16
+U32 = mybir.dt.uint32
+U8 = mybir.dt.uint8
+FP8X4 = mybir.dt.float8_e4m3fn_x4
+
+P = 128
+ITEMS, PARITIES, COMPONENTS, F_IN, F_OUT = 512, 2, 16, 512, 256
+DEGREES = 4
+DEGREE_OF = [deg for deg in range(DEGREES) for m in range(2 * deg + 1)]
+FLOPS = 2 * ITEMS * PARITIES * COMPONENTS * F_IN * F_OUT
+
+PINNED = True
+LEAD = 5
+ROUND = 4
+ROUNDS_PER_CHUNK = COMPONENTS // ROUND
+CHUNKS = (ITEMS // P) * PARITIES
+N_ROUNDS = CHUNKS * ROUNDS_PER_CHUNK
+WORDS = F_IN // 2
+
+
+def tile_dense_pa_t_kernel(tc, x, W_e, W_o, b, out):
+    nc = tc.nc
+    x_rows = x.rearrange("(g n) p c k -> g n (p c k)", n=P)
+    out_rows = out.rearrange("(g n) p c f -> g n (p c f)", n=P)
+    x_cols = COMPONENTS * F_IN
+    out_cols = COMPONENTS * F_OUT
+
+    with ExitStack() as ctx:
+        const = ctx.enter_context(tc.tile_pool(name="const", bufs=1))
+        x_pool = ctx.enter_context(tc.tile_pool(name="x_pool", bufs=LEAD))
+        out_pool = ctx.enter_context(tc.tile_pool(name="out_pool", bufs=5))
+        stage = ctx.enter_context(tc.tile_pool(name="stage", bufs=3))
+        psum_t = ctx.enter_context(tc.psum_pool(name="psum_t", bufs=4))
+        psum_o = ctx.enter_context(tc.psum_pool(name="psum_o", bufs=4))
+        if PINNED:
+            ctx.enter_context(tc.manual_schedule())
+
+        ident = const.tile([P, P], F32)
+        make_identity(nc, ident[:])
+        ones = const.tile([P, P], BF16)
+        nc.vector.memset(ones[:], 1.0)
+        b_row = const.tile([P, F_OUT], BF16)
+        nc.vector.memset(b_row[:], 0.0)
+        nc.scalar.dma_start(out=b_row[0:1, :], in_=b.rearrange("(o f) -> o f", o=1))
+
+        w_raw = const.tile([P, PARITIES * DEGREES, 4, F_OUT], BF16)
+        w_grp = const.tile([P, PARITIES * DEGREES, F_OUT, 4], BF16, align_bytes=64)
+        w_codes = const.tile([P, PARITIES * DEGREES * F_OUT], U32, align_bytes=64)
+        w_scales = const.tile([P, PARITIES * DEGREES * F_OUT], U8, align_bytes=64)
+
+        def load_w(par, w):
+            nc.sync.dma_start(
+                out=w_raw[:, par * DEGREES:(par + 1) * DEGREES].rearrange(
+                    "q l (u e) c -> q (l u) (e c)", u=2),
+                in_=w.rearrange("l (u q e) c -> q (l u) (e c)", u=2, q=P, e=2),
+            )
+
+        x_tiles = {}
+
+        def load_x(ch, pieces):
+            xt = x_pool.tile([P, x_cols], BF16, name="xt")
+            x_tiles[ch] = xt
+            g, par = divmod(ch, PARITIES)
+            step = x_cols // pieces
+            return [(xt, g, par * x_cols, i * step, step) for i in range(pieces)]
+
+        def issue(piece):
+            xt, g, base, lo, step = piece
+            nc.sync.dma_start(out=xt[:, lo:lo + step], in_=x_rows[g, :, base + lo:base + lo + step])
+
+        first = load_x(0, 4)
+        load_w(0, W_e)
+        issue(first[0])
+        issue(first[1])
+        load_w(1, W_o)
+        issue(first[2])
+        issue(first[3])
+        for ch in range(1, LEAD):
+            issue(load_x(ch, 1)[0])
+
+        bias_ps = psum_o.tile([P, 2, F_OUT], F32, name="op")
+        nc.tensor.matmul(bias_ps[:, 0, :], lhsT=ones[:], rhs=b_row[:], start=True, stop=True)
+        bias = const.tile([P, F_OUT], F32)
+        nc.vector.tensor_copy(out=bias[:], in_=bias_ps[:, 0, :])
+
+        def regroup_w(w):
+            nc.vector.tensor_copy(
+                out=w_grp[:, w].rearrange("q (c i) t -> q c t i", i=4),
+                in_=w_raw[:, w].rearrange("q t (c i) -> q c t i", i=4),
+            )
+
+        def quantise_w(pair):
+            lo = 2 * pair * F_OUT
+            nc.vector.quantize_mx(
+                out=w_codes[:, lo:lo + 2 * F_OUT].bitcast(FP8X4),
+                scales=w_scales[:, lo:lo + 2 * F_OUT],
+                in_=w_grp[:, 2 * pair:2 * pair + 2].rearrange("q w c t -> q (w c t)"),
+            )
+
+        weight_work = []
+        for pair in range(PARITIES * DEGREES // 2):
+            weight_work.append((regroup_w, 2 * pair))
+            weight_work.append((regroup_w, 2 * pair + 1))
+            weight_work.append((quantise_w, pair))
+
+        def do_weight_work(k):
+            for fn, arg in weight_work[2 * k:2 * k + 2]:
+                fn(arg)
+
+        banks, grouped, codes, scales, out_tiles = {}, {}, {}, {}, {}
+
+        def transposes(i):
+            ch, r = divmod(i, ROUNDS_PER_CHUNK)
+            words = x_tiles[ch][:].bitcast(F32)
+            pair = []
+            for h in range(2):
+                tp = psum_t.tile([P, 2, 2, P], F32, name="tp")
+                for a in range(2):
+                    c = ROUND * r + 2 * h + a
+                    for u in range(2):
+                        lo = c * WORDS + u * P
+                        nc.tensor.transpose(tp[:, a, u, :], words[:, lo:lo + P], ident[:])
+                pair.append(tp)
+            banks[i] = pair
+
+        def copies(i):
+            grp = stage.tile([P, ROUND * F_IN], BF16, name="grp", align_bytes=64)
+            grouped[i] = grp
+            words = grp[:].bitcast(F32)
+            half = ROUND * F_IN // 4
+            for h in range(2):
+                dst = words[:, h * half:(h + 1) * half].rearrange("q (a n u) -> q a n u", a=2, u=2)
+                src = banks[i][h][:].rearrange("q a u n -> q a n u")
+                if h == 0:
+                    nc.vector.tensor_copy(out=dst, in_=src)
+                else:
+                    nc.scalar.copy(out=dst, in_=src)
+
+        def quantise(i):
+            cd = stage.tile([P, ROUND * P], U32, name="cd", align_bytes=64)
+            sc = stage.tile([P, ROUND * P], U8, name="sc", align_bytes=64)
+            codes[i], scales[i] = cd, sc
+            nc.vector.quantize_mx(out=cd[:].bitcast(FP8X4), scales=sc[:], in_=grouped[i][:])
+
+        def products(i):
+            ch, r = divmod(i, ROUNDS_PER_CHUNK)
+            g, par = divmod(ch, PARITIES)
+            if r == 0:
+                ot_new = out_pool.tile([P, out_cols], F32, name="ot")
+                out_tiles[ch] = ot_new
+            ot = out_tiles[ch]
+            cd, sc = codes[i], scales[i]
+            for h in range(2):
+                op = psum_o.tile([P, 2, F_OUT], F32, name="op")
+                for a in range(2):
+                    j = 2 * h + a
+                    w = par * DEGREES + DEGREE_OF[ROUND * r + j]
+                    nc.tensor.matmul_mx(
+                        out=op[:, a, :],
+                        lhsT=cd[:, j * P:(j + 1) * P].bitcast(FP8X4),
+                        lhsT_scale=sc[:, j * P:(j + 1) * P],
+                        rhs=w_codes[:, w * F_OUT:(w + 1) * F_OUT].bitcast(FP8X4),
+                        rhs_scale=w_scales[:, w * F_OUT:(w + 1) * F_OUT],
+                        start=True,
+                        stop=True,
+                    )
+                lo = (ROUND * r + 2 * h) * F_OUT
+                if par == 0 and r == 0 and h == 0:
+                    nc.vector.tensor_tensor(out=ot[:, 0:F_OUT], in0=op[:, 0, :], in1=bias[:],
+                                            op=mybir.AluOpType.add)
+                    nc.vector.tensor_copy(out=ot[:, F_OUT:2 * F_OUT], in_=op[:, 1, :])
+                else:
+                    nc.scalar.copy(out=ot[:, lo:lo + 2 * F_OUT], in_=op[:].rearrange("q a f -> q (a f)"))
+            if r == ROUNDS_PER_CHUNK - 1:
+                nc.sync.dma_start(out=out_rows[g, :, par * out_cols:(par + 1) * out_cols], in_=ot[:])
+                if ch + LEAD < CHUNKS:
+                    issue(load_x(ch + LEAD, 1)[0])
+
+        do_weight_work(0)
+        for s in range(N_ROUNDS + 2):
+            if s < N_ROUNDS:
+                transposes(s)
+                copies(s)
+            if 1 <= s <= N_ROUNDS:
+                quantise(s - 1)
+            if s >= 2:
+                products(s - 2)
+            do_weight_work(s + 1)

@@ -54,11 +54,11 @@ def tile_dense_pa_t_kernel(tc, x, W_e, W_o, b, out):
         w_codes = const.tile([P, PARITIES * DEGREES * F_OUT], U32, align_bytes=64)
         w_scales = const.tile([P, PARITIES * DEGREES * F_OUT], U8, align_bytes=64)
 
-        def load_w(par, w):
+        def load_w(par, w, half):
+            lo = par * DEGREES + 2 * half
             nc.sync.dma_start(
-                out=w_raw[:, par * DEGREES:(par + 1) * DEGREES].rearrange(
-                    "q l (u e) c -> q (l u) (e c)", u=2),
-                in_=w.rearrange("l (u q e) c -> q (l u) (e c)", u=2, q=P, e=2),
+                out=w_raw[:, lo:lo + 2].rearrange("q l (u e) c -> q (l u) (e c)", u=2),
+                in_=w[2 * half:2 * half + 2].rearrange("l (u q e) c -> q (l u) (e c)", u=2, q=P, e=2),
             )
 
         x_tiles = {}
@@ -75,19 +75,23 @@ def tile_dense_pa_t_kernel(tc, x, W_e, W_o, b, out):
             nc.sync.dma_start(out=xt[:, lo:lo + step], in_=x_rows[g, :, base + lo:base + lo + step])
 
         first = load_x(0, 4)
-        load_w(0, W_e)
+        load_w(0, W_e, 0)
         issue(first[0])
+        load_w(0, W_e, 1)
         issue(first[1])
-        load_w(1, W_o)
+        load_w(1, W_o, 0)
         issue(first[2])
+        load_w(1, W_o, 1)
         issue(first[3])
         for ch in range(1, LEAD):
             issue(load_x(ch, 1)[0])
 
-        bias_ps = psum_o.tile([P, 2, F_OUT], F32, name="op")
-        nc.tensor.matmul(bias_ps[:, 0, :], lhsT=ones[:], rhs=b_row[:], start=True, stop=True)
         bias = const.tile([P, F_OUT], F32)
-        nc.vector.tensor_copy(out=bias[:], in_=bias_ps[:, 0, :])
+
+        def spread_bias():
+            bias_ps = psum_o.tile([P, 2, F_OUT], F32, name="op")
+            nc.tensor.matmul(bias_ps[:, 0, :], lhsT=ones[:], rhs=b_row[:], start=True, stop=True)
+            nc.vector.tensor_copy(out=bias[:], in_=bias_ps[:, 0, :])
 
         def regroup_w(w):
             nc.vector.tensor_copy(
@@ -189,6 +193,8 @@ def tile_dense_pa_t_kernel(tc, x, W_e, W_o, b, out):
                 copies(s)
             if 1 <= s <= N_ROUNDS:
                 quantise(s - 1)
+            if s == 1:
+                spread_bias()
             if s >= 2:
                 products(s - 2)
             do_weight_work(s + 1)

@@ -16,25 +16,26 @@ DEGREE_OF = [deg for deg in range(DEGREES) for m in range(2 * deg + 1)]
 FLOPS = 2 * ITEMS * PARITIES * COMPONENTS * F_IN * F_OUT
 
 PINNED = True
-LEAD = 5
+SLICES = PARITIES * COMPONENTS
+BLOCKS = ITEMS // P
 ROUND = 4
-ROUNDS_PER_CHUNK = COMPONENTS // ROUND
-CHUNKS = (ITEMS // P) * PARITIES
-N_ROUNDS = CHUNKS * ROUNDS_PER_CHUNK
+ROUNDS_PER_BLOCK = SLICES // ROUND
+N_ROUNDS = BLOCKS * ROUNDS_PER_BLOCK
 WORDS = F_IN // 2
+LEAD = 3
+FIRST_LOADS = [4, 12, 16]
+LAST_STORES = [16, 8, 8]
 
 
 def tile_dense_pa_t_kernel(tc, x, W_e, W_o, b, out):
     nc = tc.nc
     x_rows = x.rearrange("(g n) p c k -> g n (p c k)", n=P)
     out_rows = out.rearrange("(g n) p c f -> g n (p c f)", n=P)
-    x_cols = COMPONENTS * F_IN
-    out_cols = COMPONENTS * F_OUT
 
     with ExitStack() as ctx:
         const = ctx.enter_context(tc.tile_pool(name="const", bufs=1))
         x_pool = ctx.enter_context(tc.tile_pool(name="x_pool", bufs=LEAD))
-        out_pool = ctx.enter_context(tc.tile_pool(name="out_pool", bufs=5))
+        out_pool = ctx.enter_context(tc.tile_pool(name="out_pool", bufs=3))
         stage = ctx.enter_context(tc.tile_pool(name="stage", bufs=3))
         psum_t = ctx.enter_context(tc.psum_pool(name="psum_t", bufs=4))
         psum_o = ctx.enter_context(tc.psum_pool(name="psum_o", bufs=4))
@@ -49,10 +50,12 @@ def tile_dense_pa_t_kernel(tc, x, W_e, W_o, b, out):
         nc.vector.memset(b_row[:], 0.0)
         nc.scalar.dma_start(out=b_row[0:1, :], in_=b.rearrange("(o f) -> o f", o=1))
 
-        w_raw = const.tile([P, PARITIES * DEGREES, 4, F_OUT], BF16)
-        w_grp = const.tile([P, PARITIES * DEGREES, F_OUT, 4], BF16, align_bytes=64)
-        w_codes = const.tile([P, PARITIES * DEGREES * F_OUT], U32, align_bytes=64)
-        w_scales = const.tile([P, PARITIES * DEGREES * F_OUT], U8, align_bytes=64)
+        n_w = PARITIES * DEGREES
+        w_stage = out_pool.tile([P, 2, n_w, 4 * F_OUT], BF16, name="ot", align_bytes=64)
+        w_raw = w_stage[:, 0].rearrange("q w (t c) -> q w t c", t=4)
+        w_grp = w_stage[:, 1].rearrange("q w (c t) -> q w c t", t=4)
+        w_codes = const.tile([P, n_w * F_OUT], U32, align_bytes=64)
+        w_scales = const.tile([P, n_w * F_OUT], U8, align_bytes=64)
 
         def load_w(par, w, half):
             lo = par * DEGREES + 2 * half
@@ -63,28 +66,22 @@ def tile_dense_pa_t_kernel(tc, x, W_e, W_o, b, out):
 
         x_tiles = {}
 
-        def load_x(ch, pieces):
-            xt = x_pool.tile([P, x_cols], BF16, name="xt")
-            x_tiles[ch] = xt
-            g, par = divmod(ch, PARITIES)
-            step = x_cols // pieces
-            return [(xt, g, par * x_cols, i * step, step) for i in range(pieces)]
+        def load_x(g, lo, n):
+            if lo == 0:
+                xt = x_pool.tile([P, SLICES * F_IN], BF16, name="xt")
+                x_tiles[g] = xt
+            nc.sync.dma_start(out=x_tiles[g][:, lo * F_IN:(lo + n) * F_IN],
+                              in_=x_rows[g, :, lo * F_IN:(lo + n) * F_IN])
 
-        def issue(piece):
-            xt, g, base, lo, step = piece
-            nc.sync.dma_start(out=xt[:, lo:lo + step], in_=x_rows[g, :, base + lo:base + lo + step])
-
-        first = load_x(0, 4)
         load_w(0, W_e, 0)
-        issue(first[0])
+        load_x(0, 0, FIRST_LOADS[0])
         load_w(0, W_e, 1)
-        issue(first[1])
+        load_x(0, FIRST_LOADS[0], FIRST_LOADS[1])
         load_w(1, W_o, 0)
-        issue(first[2])
         load_w(1, W_o, 1)
-        issue(first[3])
-        for ch in range(1, LEAD):
-            issue(load_x(ch, 1)[0])
+        load_x(0, FIRST_LOADS[0] + FIRST_LOADS[1], FIRST_LOADS[2])
+        for g in range(1, LEAD):
+            load_x(g, 0, SLICES)
 
         bias = const.tile([P, F_OUT], F32)
 
@@ -108,7 +105,7 @@ def tile_dense_pa_t_kernel(tc, x, W_e, W_o, b, out):
             )
 
         weight_work = []
-        for pair in range(PARITIES * DEGREES // 2):
+        for pair in range(n_w // 2):
             weight_work.append((regroup_w, 2 * pair))
             weight_work.append((regroup_w, 2 * pair + 1))
             weight_work.append((quantise_w, pair))
@@ -118,17 +115,23 @@ def tile_dense_pa_t_kernel(tc, x, W_e, W_o, b, out):
                 fn(arg)
 
         banks, grouped, codes, scales, out_tiles = {}, {}, {}, {}, {}
+        store_ends = {}
+        for g in range(BLOCKS):
+            lo = 0
+            for n in (LAST_STORES if g == BLOCKS - 1 else [SLICES]):
+                store_ends[(g, lo + n)] = lo
+                lo += n
 
         def transposes(i):
-            ch, r = divmod(i, ROUNDS_PER_CHUNK)
-            words = x_tiles[ch][:].bitcast(F32)
+            g, r = divmod(i, ROUNDS_PER_BLOCK)
+            words = x_tiles[g][:].bitcast(F32)
             pair = []
             for h in range(2):
                 tp = psum_t.tile([P, 2, 2, P], F32, name="tp")
                 for a in range(2):
-                    c = ROUND * r + 2 * h + a
+                    s = ROUND * r + 2 * h + a
                     for u in range(2):
-                        lo = c * WORDS + u * P
+                        lo = s * WORDS + u * P
                         nc.tensor.transpose(tp[:, a, u, :], words[:, lo:lo + P], ident[:])
                 pair.append(tp)
             banks[i] = pair
@@ -153,18 +156,19 @@ def tile_dense_pa_t_kernel(tc, x, W_e, W_o, b, out):
             nc.vector.quantize_mx(out=cd[:].bitcast(FP8X4), scales=sc[:], in_=grouped[i][:])
 
         def products(i):
-            ch, r = divmod(i, ROUNDS_PER_CHUNK)
-            g, par = divmod(ch, PARITIES)
+            g, r = divmod(i, ROUNDS_PER_BLOCK)
             if r == 0:
-                ot_new = out_pool.tile([P, out_cols], F32, name="ot")
-                out_tiles[ch] = ot_new
-            ot = out_tiles[ch]
+                ot_new = out_pool.tile([P, SLICES * F_OUT], F32, name="ot", align_bytes=64)
+                out_tiles[g] = ot_new
+            ot = out_tiles[g]
             cd, sc = codes[i], scales[i]
             for h in range(2):
                 op = psum_o.tile([P, 2, F_OUT], F32, name="op")
+                first = ROUND * r + 2 * h
                 for a in range(2):
                     j = 2 * h + a
-                    w = par * DEGREES + DEGREE_OF[ROUND * r + j]
+                    par, c = divmod(first + a, COMPONENTS)
+                    w = par * DEGREES + DEGREE_OF[c]
                     nc.tensor.matmul_mx(
                         out=op[:, a, :],
                         lhsT=cd[:, j * P:(j + 1) * P].bitcast(FP8X4),
@@ -174,17 +178,19 @@ def tile_dense_pa_t_kernel(tc, x, W_e, W_o, b, out):
                         start=True,
                         stop=True,
                     )
-                lo = (ROUND * r + 2 * h) * F_OUT
-                if par == 0 and r == 0 and h == 0:
+                lo = first * F_OUT
+                if first == 0:
                     nc.vector.tensor_tensor(out=ot[:, 0:F_OUT], in0=op[:, 0, :], in1=bias[:],
                                             op=mybir.AluOpType.add)
                     nc.vector.tensor_copy(out=ot[:, F_OUT:2 * F_OUT], in_=op[:, 1, :])
                 else:
                     nc.scalar.copy(out=ot[:, lo:lo + 2 * F_OUT], in_=op[:].rearrange("q a f -> q (a f)"))
-            if r == ROUNDS_PER_CHUNK - 1:
-                nc.sync.dma_start(out=out_rows[g, :, par * out_cols:(par + 1) * out_cols], in_=ot[:])
-                if ch + LEAD < CHUNKS:
-                    issue(load_x(ch + LEAD, 1)[0])
+            end = ROUND * (r + 1)
+            if (g, end) in store_ends:
+                lo = store_ends[(g, end)]
+                nc.sync.dma_start(out=out_rows[g, :, lo * F_OUT:end * F_OUT], in_=ot[:, lo * F_OUT:end * F_OUT])
+                if end == SLICES and g + LEAD < BLOCKS:
+                    load_x(g + LEAD, 0, SLICES)
 
         do_weight_work(0)
         for s in range(N_ROUNDS + 2):

@@ -15,7 +15,7 @@ DEGREES = 4
 DEGREE_OF = [deg for deg in range(DEGREES) for m in range(2 * deg + 1)]
 FLOPS = 2 * ITEMS * PARITIES * COMPONENTS * F_IN * F_OUT
 
-PINNED = True
+PINNED = False
 SLICES = PARITIES * COMPONENTS
 BLOCKS = ITEMS // P
 ROUND = 4

@@ -15,7 +15,7 @@ DEGREES = 4
 DEGREE_OF = [deg for deg in range(DEGREES) for m in range(2 * deg + 1)]
 FLOPS = 2 * ITEMS * PARITIES * COMPONENTS * F_IN * F_OUT
 
-PINNED = False
+PINNED = True
 SLICES = PARITIES * COMPONENTS
 BLOCKS = ITEMS // P
 ROUND = 4
@@ -188,7 +188,7 @@ def tile_dense_pa_t_kernel(tc, x, W_e, W_o, b, out):
             end = ROUND * (r + 1)
             if (g, end) in store_ends:
                 lo = store_ends[(g, end)]
-                nc.sync.dma_start(out=out_rows[g, :, lo * F_OUT:end * F_OUT], in_=ot[:, lo * F_OUT:end * F_OUT])
+                nc.scalar.dma_start(out=out_rows[g, :, lo * F_OUT:end * F_OUT], in_=ot[:, lo * F_OUT:end * F_OUT])
                 if end == SLICES and g + LEAD < BLOCKS:
                     load_x(g + LEAD, 0, SLICES)
 

@@ -15,7 +15,7 @@ DEGREES = 4
 DEGREE_OF = [deg for deg in range(DEGREES) for m in range(2 * deg + 1)]
 FLOPS = 2 * ITEMS * PARITIES * COMPONENTS * F_IN * F_OUT
 
-PINNED = True
+PINNED = False
 SLICES = PARITIES * COMPONENTS
 BLOCKS = ITEMS // P
 ROUND = 4
@@ -60,8 +60,8 @@ def tile_dense_pa_t_kernel(tc, x, W_e, W_o, b, out):
         def load_w(par, w, half):
             lo = par * DEGREES + 2 * half
             nc.sync.dma_start(
-                out=w_raw[:, lo:lo + 2].rearrange("q l (u e) c -> q (l u) (e c)", u=2),
-                in_=w[2 * half:2 * half + 2].rearrange("l (u q e) c -> q (l u) (e c)", u=2, q=P, e=2),
+                out=w_raw[:, lo:lo + 2].rearrange("q l t c -> q l (t c)"),
+                in_=w[2 * half:2 * half + 2].rearrange("l (q t) c -> q l (t c)", t=4),
             )
 
         x_tiles = {}
@@ -131,8 +131,7 @@ def tile_dense_pa_t_kernel(tc, x, W_e, W_o, b, out):
                 for a in range(2):
                     s = ROUND * r + 2 * h + a
                     for u in range(2):
-                        lo = s * WORDS + u * P
-                        nc.tensor.transpose(tp[:, a, u, :], words[:, lo:lo + P], ident[:])
+                        nc.tensor.transpose(tp[:, a, u, :], words[:, s * WORDS + u:(s + 1) * WORDS:2], ident[:])
                 pair.append(tp)
             banks[i] = pair
 
@@ -188,7 +187,7 @@ def tile_dense_pa_t_kernel(tc, x, W_e, W_o, b, out):
             end = ROUND * (r + 1)
             if (g, end) in store_ends:
                 lo = store_ends[(g, end)]
-                nc.scalar.dma_start(out=out_rows[g, :, lo * F_OUT:end * F_OUT], in_=ot[:, lo * F_OUT:end * F_OUT])
+                nc.sync.dma_start(out=out_rows[g, :, lo * F_OUT:end * F_OUT], in_=ot[:, lo * F_OUT:end * F_OUT])
                 if end == SLICES and g + LEAD < BLOCKS:
                     load_x(g + LEAD, 0, SLICES)
 

@@ -15,15 +15,14 @@ DEGREES = 4
 DEGREE_OF = [deg for deg in range(DEGREES) for m in range(2 * deg + 1)]
 FLOPS = 2 * ITEMS * PARITIES * COMPONENTS * F_IN * F_OUT
 
-PINNED = False
 SLICES = PARITIES * COMPONENTS
 BLOCKS = ITEMS // P
 ROUND = 4
 ROUNDS_PER_BLOCK = SLICES // ROUND
 N_ROUNDS = BLOCKS * ROUNDS_PER_BLOCK
 WORDS = F_IN // 2
-LEAD = 3
-FIRST_LOADS = [4, 12, 16]
+BIG_ALIGN = 4096
+BIG_BUFS = 6
 LAST_STORES = [16, 8, 8]
 
 
@@ -34,13 +33,11 @@ def tile_dense_pa_t_kernel(tc, x, W_e, W_o, b, out):
 
     with ExitStack() as ctx:
         const = ctx.enter_context(tc.tile_pool(name="const", bufs=1))
-        x_pool = ctx.enter_context(tc.tile_pool(name="x_pool", bufs=LEAD))
-        out_pool = ctx.enter_context(tc.tile_pool(name="out_pool", bufs=3))
+        big = ctx.enter_context(tc.tile_pool(name="big", bufs=BIG_BUFS))
         stage = ctx.enter_context(tc.tile_pool(name="stage", bufs=3))
         psum_t = ctx.enter_context(tc.psum_pool(name="psum_t", bufs=4))
         psum_o = ctx.enter_context(tc.psum_pool(name="psum_o", bufs=4))
-        if PINNED:
-            ctx.enter_context(tc.manual_schedule())
+        ctx.enter_context(tc.manual_schedule(engines={mybir.EngineType.SP}))
 
         ident = const.tile([P, P], F32)
         make_identity(nc, ident[:])
@@ -51,7 +48,7 @@ def tile_dense_pa_t_kernel(tc, x, W_e, W_o, b, out):
         nc.scalar.dma_start(out=b_row[0:1, :], in_=b.rearrange("(o f) -> o f", o=1))
 
         n_w = PARITIES * DEGREES
-        w_stage = out_pool.tile([P, 2, n_w, 4 * F_OUT], BF16, name="ot", align_bytes=64)
+        w_stage = big.tile([P, 2, n_w, 4 * F_OUT], BF16, name="blk", align_bytes=BIG_ALIGN)
         w_raw = w_stage[:, 0].rearrange("q w (t c) -> q w t c", t=4)
         w_grp = w_stage[:, 1].rearrange("q w (c t) -> q w c t", t=4)
         w_codes = const.tile([P, n_w * F_OUT], U32, align_bytes=64)
@@ -68,19 +65,20 @@ def tile_dense_pa_t_kernel(tc, x, W_e, W_o, b, out):
 
         def load_x(g, lo, n):
             if lo == 0:
-                xt = x_pool.tile([P, SLICES * F_IN], BF16, name="xt")
+                xt = big.tile([P, SLICES * F_IN], BF16, name="blk", align_bytes=BIG_ALIGN)
                 x_tiles[g] = xt
             nc.sync.dma_start(out=x_tiles[g][:, lo * F_IN:(lo + n) * F_IN],
                               in_=x_rows[g, :, lo * F_IN:(lo + n) * F_IN])
 
+        load_x(0, 0, 4)
         load_w(0, W_e, 0)
-        load_x(0, 0, FIRST_LOADS[0])
+        load_x(0, 4, 4)
         load_w(0, W_e, 1)
-        load_x(0, FIRST_LOADS[0], FIRST_LOADS[1])
+        load_x(0, 8, 8)
         load_w(1, W_o, 0)
         load_w(1, W_o, 1)
-        load_x(0, FIRST_LOADS[0] + FIRST_LOADS[1], FIRST_LOADS[2])
-        for g in range(1, LEAD):
+        load_x(0, 16, 16)
+        for g in range(1, BLOCKS):
             load_x(g, 0, SLICES)
 
         bias = const.tile([P, F_OUT], F32)
@@ -157,7 +155,7 @@ def tile_dense_pa_t_kernel(tc, x, W_e, W_o, b, out):
         def products(i):
             g, r = divmod(i, ROUNDS_PER_BLOCK)
             if r == 0:
-                ot_new = out_pool.tile([P, SLICES * F_OUT], F32, name="ot", align_bytes=64)
+                ot_new = big.tile([P, SLICES * F_OUT], F32, name="blk", align_bytes=BIG_ALIGN)
                 out_tiles[g] = ot_new
             ot = out_tiles[g]
             cd, sc = codes[i], scales[i]
@@ -188,8 +186,6 @@ def tile_dense_pa_t_kernel(tc, x, W_e, W_o, b, out):
             if (g, end) in store_ends:
                 lo = store_ends[(g, end)]
                 nc.sync.dma_start(out=out_rows[g, :, lo * F_OUT:end * F_OUT], in_=ot[:, lo * F_OUT:end * F_OUT])
-                if end == SLICES and g + LEAD < BLOCKS:
-                    load_x(g + LEAD, 0, SLICES)
 
         do_weight_work(0)
         for s in range(N_ROUNDS + 2):

@@ -37,7 +37,7 @@ def tile_dense_pa_t_kernel(tc, x, W_e, W_o, b, out):
         stage = ctx.enter_context(tc.tile_pool(name="stage", bufs=3))
         psum_t = ctx.enter_context(tc.psum_pool(name="psum_t", bufs=4))
         psum_o = ctx.enter_context(tc.psum_pool(name="psum_o", bufs=4))
-        ctx.enter_context(tc.manual_schedule(engines={mybir.EngineType.SP}))
+        ctx.enter_context(tc.manual_schedule())
 
         ident = const.tile([P, P], F32)
         make_identity(nc, ident[:])

@@ -45,7 +45,6 @@ def tile_dense_pa_t_kernel(tc, x, W_e, W_o, b, out):
         nc.vector.memset(ones[:], 1.0)
         b_row = const.tile([P, F_OUT], BF16)
         nc.vector.memset(b_row[:], 0.0)
-        nc.scalar.dma_start(out=b_row[0:1, :], in_=b.rearrange("(o f) -> o f", o=1))
 
         n_w = PARITIES * DEGREES
         w_stage = big.tile([P, 2, n_w, 4 * F_OUT], BF16, name="blk", align_bytes=BIG_ALIGN)
@@ -72,6 +71,7 @@ def tile_dense_pa_t_kernel(tc, x, W_e, W_o, b, out):
 
         load_x(0, 0, 4)
         load_w(0, W_e, 0)
+        nc.sync.dma_start(out=b_row[0:1, :], in_=b.rearrange("(o f) -> o f", o=1))
         load_x(0, 4, 4)
         load_w(0, W_e, 1)
         load_x(0, 8, 8)

@@ -55,7 +55,7 @@ def tile_dense_pa_t_kernel(tc, x, W_e, W_o, b, out):
 
         def load_w(par, w, half):
             lo = par * DEGREES + 2 * half
-            nc.sync.dma_start(
+            nc.scalar.dma_start(
                 out=w_raw[:, lo:lo + 2].rearrange("q l t c -> q l (t c)"),
                 in_=w[2 * half:2 * half + 2].rearrange("l (q t) c -> q l (t c)", t=4),
             )

@@ -1,7 +1,6 @@
 from contextlib import ExitStack
 
 import concourse.mybir as mybir
-from concourse.masks import make_identity
 
 F32 = mybir.dt.float32
 BF16 = mybir.dt.bfloat16
@@ -39,8 +38,20 @@ def tile_dense_pa_t_kernel(tc, x, W_e, W_o, b, out):
         psum_o = ctx.enter_context(tc.psum_pool(name="psum_o", bufs=4))
         ctx.enter_context(tc.manual_schedule())
 
+        ones_f = const.tile([P, P], F32, align_bytes=64)
+        nc.vector.memset(ones_f[:], 1.0)
+        col = const.tile([P, P], F32, align_bytes=64)
+        nc.vector.tensor_tensor_scan(out=col[:], data0=ones_f[:], data1=ones_f[:], initial=0.0,
+                                     op0=mybir.AluOpType.mult, op1=mybir.AluOpType.add)
+        col_t = const.tile([P, P], F32, align_bytes=64)
+        nc.vector.transpose(out=col_t[:], in_=col[:])
+        same = const.tile([P, P], F32, align_bytes=64)
+        nc.vector.tensor_tensor(out=same[:], in0=col_t[:], in1=col[:], op=mybir.AluOpType.is_equal)
         ident = const.tile([P, P], F32)
-        make_identity(nc, ident[:])
+        nc.vector.memset(ident[:], 0.0)
+        for quad in range(4):
+            box = slice(32 * quad, 32 * quad + 32)
+            nc.vector.tensor_copy(out=ident[box, box], in_=same[box, box])
         ones = const.tile([P, P], BF16)
         nc.vector.memset(ones[:], 1.0)
         b_row = const.tile([P, F_OUT], BF16)

@@ -27,8 +27,8 @@ LAST_STORES = [16, 8, 8]
 
 def tile_dense_pa_t_kernel(tc, x, W_e, W_o, b, out):
     nc = tc.nc
-    x_rows = x.rearrange("(g n) p c k -> g n (p c k)", n=P)
-    out_rows = out.rearrange("(g n) p c f -> g n (p c f)", n=P)
+    x_rows = x.rearrange("(n g) p c k -> g n (p c k)", n=P)
+    out_rows = out.rearrange("(n g) p c f -> g n (p c f)", n=P)
 
     with ExitStack() as ctx:
         const = ctx.enter_context(tc.tile_pool(name="const", bufs=1))

@@ -64,11 +64,11 @@ def tile_dense_pa_t_kernel(tc, x, W_e, W_o, b, out):
         w_codes = const.tile([P, n_w * F_OUT], U32, align_bytes=64)
         w_scales = const.tile([P, n_w * F_OUT], U8, align_bytes=64)
 
-        def load_w(par, w, half):
-            lo = par * DEGREES + 2 * half
+        def load_w(par, w):
+            lo = par * DEGREES
             nc.scalar.dma_start(
-                out=w_raw[:, lo:lo + 2].rearrange("q l t c -> q l (t c)"),
-                in_=w[2 * half:2 * half + 2].rearrange("l (q t) c -> q l (t c)", t=4),
+                out=w_raw[:, lo:lo + DEGREES].rearrange("q l t c -> q l (t c)"),
+                in_=w.rearrange("l (q t) c -> q l (t c)", t=4),
             )
 
         x_tiles = {}
@@ -80,14 +80,11 @@ def tile_dense_pa_t_kernel(tc, x, W_e, W_o, b, out):
             nc.sync.dma_start(out=x_tiles[g][:, lo * F_IN:(lo + n) * F_IN],
                               in_=x_rows[g, :, lo * F_IN:(lo + n) * F_IN])
 
-        load_x(0, 0, 4)
-        load_w(0, W_e, 0)
+        load_x(0, 0, 8)
+        load_w(0, W_e)
         nc.sync.dma_start(out=b_row[0:1, :], in_=b.rearrange("(o f) -> o f", o=1))
-        load_x(0, 4, 4)
-        load_w(0, W_e, 1)
         load_x(0, 8, 8)
-        load_w(1, W_o, 0)
-        load_w(1, W_o, 1)
+        load_w(1, W_o)
         load_x(0, 16, 16)
         for g in range(1, BLOCKS):
             load_x(g, 0, SLICES)

from contextlib import ExitStack

import concourse.mybir as mybir

F32 = mybir.dt.float32
BF16 = mybir.dt.bfloat16
U32 = mybir.dt.uint32
U8 = mybir.dt.uint8
FP8X4 = mybir.dt.float8_e4m3fn_x4

P = 128
ITEMS, PARITIES, COMPONENTS, F_IN, F_OUT = 512, 2, 16, 512, 256
DEGREES = 4
DEGREE_OF = [deg for deg in range(DEGREES) for m in range(2 * deg + 1)]
FLOPS = 2 * ITEMS * PARITIES * COMPONENTS * F_IN * F_OUT

SLICES = PARITIES * COMPONENTS
BLOCKS = ITEMS // P
ROUND = 4
ROUNDS_PER_BLOCK = SLICES // ROUND
N_ROUNDS = BLOCKS * ROUNDS_PER_BLOCK
WORDS = F_IN // 2
BIG_ALIGN = 4096
BIG_BUFS = 6
LAST_STORES = [16, 8, 8]


def tile_dense_pa_t_kernel(tc, x, W_e, W_o, b, out):
    nc = tc.nc
    x_rows = x.rearrange("(n g) p c k -> g n (p c k)", n=P)
    out_rows = out.rearrange("(n g) p c f -> g n (p c f)", n=P)

    with ExitStack() as ctx:
        const = ctx.enter_context(tc.tile_pool(name="const", bufs=1))
        big = ctx.enter_context(tc.tile_pool(name="big", bufs=BIG_BUFS))
        stage = ctx.enter_context(tc.tile_pool(name="stage", bufs=3))
        psum_t = ctx.enter_context(tc.psum_pool(name="psum_t", bufs=4))
        psum_o = ctx.enter_context(tc.psum_pool(name="psum_o", bufs=4))
        ctx.enter_context(tc.manual_schedule())

        ones_f = const.tile([P, P], F32, align_bytes=64)
        nc.vector.memset(ones_f[:], 1.0)
        col = const.tile([P, P], F32, align_bytes=64)
        nc.vector.tensor_tensor_scan(out=col[:], data0=ones_f[:], data1=ones_f[:], initial=0.0,
                                     op0=mybir.AluOpType.mult, op1=mybir.AluOpType.add)
        col_t = const.tile([P, P], F32, align_bytes=64)
        nc.vector.transpose(out=col_t[:], in_=col[:])
        same = const.tile([P, P], F32, align_bytes=64)
        nc.vector.tensor_tensor(out=same[:], in0=col_t[:], in1=col[:], op=mybir.AluOpType.is_equal)
        ident = const.tile([P, P], F32)
        nc.vector.memset(ident[:], 0.0)
        for quad in range(4):
            box = slice(32 * quad, 32 * quad + 32)
            nc.vector.tensor_copy(out=ident[box, box], in_=same[box, box])
        ones = const.tile([P, P], BF16)
        nc.vector.memset(ones[:], 1.0)
        b_row = const.tile([P, F_OUT], BF16)
        nc.vector.memset(b_row[:], 0.0)

        n_w = PARITIES * DEGREES
        w_stage = big.tile([P, 2, n_w, 4 * F_OUT], BF16, name="blk", align_bytes=BIG_ALIGN)
        w_raw = w_stage[:, 0].rearrange("q w (t c) -> q w t c", t=4)
        w_grp = w_stage[:, 1].rearrange("q w (c t) -> q w c t", t=4)
        w_codes = const.tile([P, n_w * F_OUT], U32, align_bytes=64)
        w_scales = const.tile([P, n_w * F_OUT], U8, align_bytes=64)

        def load_w(par, w):
            lo = par * DEGREES
            nc.scalar.dma_start(
                out=w_raw[:, lo:lo + DEGREES].rearrange("q l t c -> q l (t c)"),
                in_=w.rearrange("l (q t) c -> q l (t c)", t=4),
            )

        x_tiles = {}

        def load_x(g, lo, n):
            if lo == 0:
                xt = big.tile([P, SLICES * F_IN], BF16, name="blk", align_bytes=BIG_ALIGN)
                x_tiles[g] = xt
            nc.sync.dma_start(out=x_tiles[g][:, lo * F_IN:(lo + n) * F_IN],
                              in_=x_rows[g, :, lo * F_IN:(lo + n) * F_IN])

        load_x(0, 0, 8)
        load_w(0, W_e)
        nc.sync.dma_start(out=b_row[0:1, :], in_=b.rearrange("(o f) -> o f", o=1))
        load_x(0, 8, 8)
        load_w(1, W_o)
        load_x(0, 16, 16)
        for g in range(1, BLOCKS):
            load_x(g, 0, SLICES)

        bias = const.tile([P, F_OUT], F32)

        def spread_bias():
            bias_ps = psum_o.tile([P, 2, F_OUT], F32, name="op")
            nc.tensor.matmul(bias_ps[:, 0, :], lhsT=ones[:], rhs=b_row[:], start=True, stop=True)
            nc.vector.tensor_copy(out=bias[:], in_=bias_ps[:, 0, :])

        def regroup_w(w):
            nc.vector.tensor_copy(
                out=w_grp[:, w].rearrange("q (c i) t -> q c t i", i=4),
                in_=w_raw[:, w].rearrange("q t (c i) -> q c t i", i=4),
            )

        def quantise_w(pair):
            lo = 2 * pair * F_OUT
            nc.vector.quantize_mx(
                out=w_codes[:, lo:lo + 2 * F_OUT].bitcast(FP8X4),
                scales=w_scales[:, lo:lo + 2 * F_OUT],
                in_=w_grp[:, 2 * pair:2 * pair + 2].rearrange("q w c t -> q (w c t)"),
            )

        weight_work = []
        for pair in range(n_w // 2):
            weight_work.append((regroup_w, 2 * pair))
            weight_work.append((regroup_w, 2 * pair + 1))
            weight_work.append((quantise_w, pair))

        def do_weight_work(k):
            for fn, arg in weight_work[2 * k:2 * k + 2]:
                fn(arg)

        banks, grouped, codes, scales, out_tiles = {}, {}, {}, {}, {}
        store_ends = {}
        for g in range(BLOCKS):
            lo = 0
            for n in (LAST_STORES if g == BLOCKS - 1 else [SLICES]):
                store_ends[(g, lo + n)] = lo
                lo += n

        def transposes(i):
            g, r = divmod(i, ROUNDS_PER_BLOCK)
            words = x_tiles[g][:].bitcast(F32)
            pair = []
            for h in range(2):
                tp = psum_t.tile([P, 2, 2, P], F32, name="tp")
                for a in range(2):
                    s = ROUND * r + 2 * h + a
                    for u in range(2):
                        nc.tensor.transpose(tp[:, a, u, :], words[:, s * WORDS + u:(s + 1) * WORDS:2], ident[:])
                pair.append(tp)
            banks[i] = pair

        def copies(i):
            grp = stage.tile([P, ROUND * F_IN], BF16, name="grp", align_bytes=64)
            grouped[i] = grp
            words = grp[:].bitcast(F32)
            half = ROUND * F_IN // 4
            for h in range(2):
                dst = words[:, h * half:(h + 1) * half].rearrange("q (a n u) -> q a n u", a=2, u=2)
                src = banks[i][h][:].rearrange("q a u n -> q a n u")
                if h == 0:
                    nc.vector.tensor_copy(out=dst, in_=src)
                else:
                    nc.scalar.copy(out=dst, in_=src)

        def quantise(i):
            cd = stage.tile([P, ROUND * P], U32, name="cd", align_bytes=64)
            sc = stage.tile([P, ROUND * P], U8, name="sc", align_bytes=64)
            codes[i], scales[i] = cd, sc
            nc.vector.quantize_mx(out=cd[:].bitcast(FP8X4), scales=sc[:], in_=grouped[i][:])

        def products(i):
            g, r = divmod(i, ROUNDS_PER_BLOCK)
            if r == 0:
                ot_new = big.tile([P, SLICES * F_OUT], F32, name="blk", align_bytes=BIG_ALIGN)
                out_tiles[g] = ot_new
            ot = out_tiles[g]
            cd, sc = codes[i], scales[i]
            for h in range(2):
                op = psum_o.tile([P, 2, F_OUT], F32, name="op")
                first = ROUND * r + 2 * h
                for a in range(2):
                    j = 2 * h + a
                    par, c = divmod(first + a, COMPONENTS)
                    w = par * DEGREES + DEGREE_OF[c]
                    nc.tensor.matmul_mx(
                        out=op[:, a, :],
                        lhsT=cd[:, j * P:(j + 1) * P].bitcast(FP8X4),
                        lhsT_scale=sc[:, j * P:(j + 1) * P],
                        rhs=w_codes[:, w * F_OUT:(w + 1) * F_OUT].bitcast(FP8X4),
                        rhs_scale=w_scales[:, w * F_OUT:(w + 1) * F_OUT],
                        start=True,
                        stop=True,
                    )
                lo = first * F_OUT
                if first == 0:
                    nc.vector.tensor_tensor(out=ot[:, 0:F_OUT], in0=op[:, 0, :], in1=bias[:],
                                            op=mybir.AluOpType.add)
                    nc.vector.tensor_copy(out=ot[:, F_OUT:2 * F_OUT], in_=op[:, 1, :])
                else:
                    nc.scalar.copy(out=ot[:, lo:lo + 2 * F_OUT], in_=op[:].rearrange("q a f -> q (a f)"))
            end = ROUND * (r + 1)
            if (g, end) in store_ends:
                lo = store_ends[(g, end)]
                nc.sync.dma_start(out=out_rows[g, :, lo * F_OUT:end * F_OUT], in_=ot[:, lo * F_OUT:end * F_OUT])

        do_weight_work(0)
        for s in range(N_ROUNDS + 2):
            if s < N_ROUNDS:
                transposes(s)
                copies(s)
            if 1 <= s <= N_ROUNDS:
                quantise(s - 1)
            if s == 1:
                spread_bias()
            if s >= 2:
                products(s - 2)
            do_weight_work(s + 1)
